import numpy as np
import ml_dtypes


def mxq(x, axis, fmt="e4m3"):
    dtype, down = {"e4m3": (ml_dtypes.float8_e4m3fn, 7), "e5m2": (ml_dtypes.float8_e5m2, 14)}[fmt]
    v = np.moveaxis(np.asarray(x, np.float32).astype(ml_dtypes.bfloat16).astype(np.float64), axis, -1)
    blocks = v.reshape(v.shape[:-1] + (-1, 32))
    amax = np.abs(blocks).max(-1, keepdims=True)
    byte = np.maximum(np.where(amax > 0, np.frexp(amax)[1] - 1 + 127, 0) - down, 1)
    scale = np.exp2(byte - 127.0)
    codes = (blocks / scale).astype(np.float32).astype(dtype).astype(np.float64)
    return np.moveaxis((codes * scale).reshape(v.shape), -1, axis)


WIDE = False


def mx_kscale(k):
    if not WIDE:
        return np.ones(k)
    levels = np.array([10, -10, 5, -5, 0])
    a = np.random.permutation(np.resize(levels, k // 512 * 4)).reshape(k // 512, 4)
    idx = np.arange(k)
    return np.exp2(a[idx // 512, idx % 128 // 32])


BF16 = ml_dtypes.bfloat16


def bf(x):
    return np.asarray(x, np.float32).astype(BF16)


def f64(x):
    return np.asarray(x).astype(np.float64)


E2M1 = np.array([0.0, 0.5, 1.0, 1.5, 2.0, 3.0, 4.0, 6.0, -0.0, -0.5, -1.0, -1.5, -2.0, -3.0, -4.0, -6.0])


def pack_weight(w, fmt):
    k, n = w.shape
    w = f64(bf(w)).reshape(k // 32, 32, n)
    amax = np.abs(w).max(1)
    if fmt == "e4m3":
        byte = np.frexp(amax)[1] - 1 + 127 - 7
    else:
        mant, ex = np.frexp(amax / 6.0)
        byte = np.where(mant > 0.5, ex, ex - 1) + 127
    byte = np.clip(np.where(amax > 0, byte, 1), 1, 254)
    scaled = (w * np.exp2(127.0 - byte)[:, None, :]).reshape(k, n).astype(np.float32)
    by_word = np.ascontiguousarray(scaled.reshape(k // 512, 128, 4, n).transpose(0, 1, 3, 2))
    if fmt == "e4m3":
        words = by_word.astype(ml_dtypes.float8_e4m3fn).view(np.uint8)
    else:
        c = by_word.astype(ml_dtypes.float4_e2m1fn).view(np.uint8) & 0xF
        words = c[..., 0::2] | (c[..., 1::2] << 4)
    return np.ascontiguousarray(words), np.ascontiguousarray(byte.astype(np.uint8).reshape(k // 512, 16, n))


def unpack_weight(words, scales, fmt):
    g, p, n, _ = words.shape
    if fmt == "e4m3":
        vals = np.ascontiguousarray(words).view(ml_dtypes.float8_e4m3fn).astype(np.float64)
    else:
        nib = np.empty((g, p, n, 4), np.uint8)
        nib[..., 0::2] = words & 0xF
        nib[..., 1::2] = words >> 4
        vals = E2M1[nib]
    vals = vals * np.repeat(np.exp2(scales.astype(np.float64) - 127.0), 8, axis=1)[..., None]
    return vals.transpose(0, 1, 3, 2).reshape(g * 512, n)


B, D, O1, O2, O3 = 1024, 1536, 1024, 512, 128
EPS = 1e-5
FMT = "e4m3"


def mish(v):
    return v * np.tanh(np.log(1.0 + np.exp(v)))


def ln(u, g, b):
    mu = u.mean(-1, keepdims=True)
    var = np.square(u - mu).mean(-1, keepdims=True)
    return (u - mu) * (1.0 / np.sqrt(var + EPS)) * g + b


def setup_inputs():
    s = mx_kscale(D)
    x = bf(np.random.uniform(0.0, 1.0, (B, D)) * s)
    w1 = np.random.standard_normal((O1, D)) * 1.5 / np.sqrt(D) / s
    W1_words, W1_scales = pack_weight(np.ascontiguousarray(w1.T), FMT)
    g1 = bf(1.0 + 0.1 * np.random.standard_normal(O1))
    b1 = bf(0.1 * np.random.standard_normal(O1))
    w2 = np.random.standard_normal((O2, O1)) * 1.5 / np.sqrt(O1)
    W2_words, W2_scales = pack_weight(np.ascontiguousarray(w2.T), FMT)
    g2 = bf(1.0 + 0.1 * np.random.standard_normal(O2))
    b2 = bf(0.1 * np.random.standard_normal(O2))
    return {"x": x,
            "W1_words": W1_words,
            "W1_scales": W1_scales,
            "g1": g1,
            "b1": b1,
            "W2_words": W2_words,
            "W2_scales": W2_scales,
            "g2": g2,
            "b2": b2}


def reference(x, W1_words, W1_scales, g1, b1, W2_words, W2_scales, g2, b2):
    u1 = mxq(f64(x), 1, "e4m3") @ unpack_weight(W1_words, W1_scales, FMT)
    h1 = mish(ln(u1, f64(g1), f64(b1)))
    u2 = mxq(h1, 1, "e4m3") @ unpack_weight(W2_words, W2_scales, FMT)
    return mish(ln(u2, f64(g2), f64(b2)))

@@ -1,0 +1,288 @@
+from contextlib import ExitStack
+
+import concourse.mybir as mybir
+from concourse.masks import make_identity
+
+F32 = mybir.dt.float32
+BF16 = mybir.dt.bfloat16
+I32 = mybir.dt.int32
+U32 = mybir.dt.uint32
+U8 = mybir.dt.uint8
+FP8X4 = mybir.dt.float8_e4m3fn_x4
+ALU = mybir.AluOpType
+ACT = mybir.ActivationFunctionType
+
+P = 128
+PACK = 4
+K_PASS = P * PACK
+BANK = 512
+BATCH, D_IN, D_HID, D_OUT = 1024, 1536, 1024, 512
+N_TILES = BATCH // P
+N_PAIRS = N_TILES // 2
+PASSES_1 = D_IN // K_PASS
+PASSES_2 = D_HID // K_PASS
+WORDS = K_PASS // 2
+CHUNK = 4
+N_CHUNKS = N_TILES // CHUNK
+LAG = CHUNK - 1
+EPS = 1e-5
+CAP = 40.0
+FLOPS = 2 * BATCH * D_IN * D_HID + 2 * BATCH * D_HID * D_OUT
+
+assert LAG == 3
+
+
+def tile_autoencoder_pa_kernel(
+    tc, x, W1_words, W1_scales, g1, b1, W2_words, W2_scales, g2, b2, out
+):
+    nc = tc.nc
+    with ExitStack() as ctx:
+        keep = ctx.enter_context(tc.tile_pool(name="keep", bufs=1))
+        stage = ctx.enter_context(tc.tile_pool(name="stage", bufs=2))
+        small = ctx.enter_context(tc.tile_pool(name="small", bufs=4))
+        rows = ctx.enter_context(tc.tile_pool(name="rows", bufs=N_TILES))
+        psum = ctx.enter_context(tc.psum_pool(name="psum", bufs=2))
+        ctx.enter_context(tc.manual_schedule())
+
+        identity = keep.tile([P, P], F32, name="identity")
+        make_identity(nc, identity[:])
+        one = keep.tile([P, 1], F32, name="one")
+        nc.gpsimd.memset(one[:], 1.0)
+        minus_half = keep.tile([P, 1], F32, name="minus_half")
+        nc.gpsimd.memset(minus_half[:], -0.5)
+
+        gain = {1: keep.tile([P, D_HID], BF16, name="gain1"), 2: keep.tile([P, D_OUT], BF16, name="gain2")}
+        shift = {1: keep.tile([P, D_HID], BF16, name="shift1"), 2: keep.tile([P, D_OUT], BF16, name="shift2")}
+        nc.gpsimd.dma_start(out=gain[1][:], in_=g1.partition_broadcast(P))
+        nc.gpsimd.dma_start(out=shift[1][:], in_=b1.partition_broadcast(P))
+        nc.gpsimd.dma_start(out=gain[2][:], in_=g2.partition_broadcast(P))
+        nc.gpsimd.dma_start(out=shift[2][:], in_=b2.partition_broadcast(P))
+
+        w1_codes = keep.tile([P, PASSES_1, D_HID], U32, name="w1_codes", align_bytes=64)
+        w1_scales = keep.tile([P, PASSES_1, D_HID], U8, name="w1_scales", align_bytes=64)
+        w2_codes = keep.tile([P, PASSES_2, D_OUT], U32, name="w2_codes", align_bytes=64)
+        w2_scales = keep.tile([P, PASSES_2, D_OUT], U8, name="w2_scales", align_bytes=64)
+        nc.vector.memset(w1_scales[:].rearrange("p g n -> p (g n)").bitcast(I32), 0)
+        nc.vector.memset(w2_scales[:].rearrange("p g n -> p (g n)").bitcast(I32), 0)
+
+        x_sb = keep.tile([P, N_TILES, D_IN], BF16, name="x_sb")
+
+        def load_x(i):
+            nc.sync.dma_start(out=x_sb[:, i, :], in_=x[i * P : (i + 1) * P, :])
+
+        def load_scales(plane, scales):
+            for quadrant in range(4):
+                nc.sync.dma_start(
+                    out=plane[32 * quadrant : 32 * quadrant + 4, :, :].bitcast(I32),
+                    in_=scales[:, 4 * quadrant : 4 * quadrant + 4, :].rearrange("g r n -> r g n").bitcast(I32),
+                )
+
+        def load_codes(codes, words, g):
+            nc.sync.dma_start(
+                out=codes[:, g, :].bitcast(I32),
+                in_=words[g].rearrange("p n t -> p (n t)").bitcast(I32),
+            )
+
+        load_x(0)
+        load_x(1)
+        load_scales(w1_scales, W1_scales)
+        for g in range(PASSES_1):
+            load_codes(w1_codes, W1_words, g)
+        for i in range(2, N_TILES):
+            load_x(i)
+        load_scales(w2_scales, W2_scales)
+        for g in range(PASSES_2):
+            load_codes(w2_codes, W2_words, g)
+
+        x_codes = keep.tile([P, N_PAIRS, PASSES_1, 2 * P], U32, name="x_codes", align_bytes=64)
+        x_scales = keep.tile([P, N_PAIRS, PASSES_1, 2 * P], U8, name="x_scales", align_bytes=64)
+        h_codes = keep.tile([P, N_TILES, PASSES_2 * P], U32, name="h_codes", align_bytes=64)
+        h_scales = keep.tile([P, N_TILES, PASSES_2 * P], U8, name="h_scales", align_bytes=64)
+
+        banks = {}
+        rstd_of = {}
+        pre = {}
+        act = {}
+        h_grouped = {}
+
+        def turn(bank_block, words, g):
+            for u in range(2):
+                nc.tensor.transpose(
+                    bank_block[:, u, :], words[:, WORDS * g + u : WORDS * (g + 1) : 2], identity[:]
+                )
+
+        def turn_x_pair(k):
+            grouped = stage.tile([P, PASSES_1, 2 * P * PACK], BF16, name="x_grouped", align_bytes=64)
+            for g in range(PASSES_1):
+                turned = psum.tile([P, 2, 2, P], F32, name="turned")
+                for j in range(2):
+                    turn(turned[:, j, :, :], x_sb[:, 2 * k + j, :].bitcast(F32), g)
+                nc.scalar.copy(
+                    out=grouped[:, g, :].bitcast(F32).rearrange("p (j r u) -> p j r u", j=2, u=2),
+                    in_=turned[:].rearrange("p j u r -> p j r u"),
+                )
+            return grouped
+
+        def quantise_x_pair(k, grouped):
+            for g in range(PASSES_1):
+                nc.vector.quantize_mx(
+                    out=x_codes[:, k, g, :].bitcast(FP8X4), scales=x_scales[:, k, g, :], in_=grouped[:, g, :]
+                )
+
+        def first_layer(i):
+            tile_cols = slice((i % 2) * P, (i % 2 + 1) * P)
+            banks[(1, i)] = []
+            for n in range(D_HID // BANK):
+                n_cols = slice(n * BANK, (n + 1) * BANK)
+                acc = psum.tile([P, BANK], F32, name="u1_%d" % n)
+                for g in range(PASSES_1):
+                    nc.tensor.matmul_mx(
+                        out=acc[:],
+                        lhsT=x_codes[:, i // 2, g, tile_cols].bitcast(FP8X4),
+                        lhsT_scale=x_scales[:, i // 2, g, tile_cols],
+                        rhs=w1_codes[:, g, n_cols].bitcast(FP8X4),
+                        rhs_scale=w1_scales[:, g, n_cols],
+                        start=(g == 0),
+                        stop=(g == PASSES_1 - 1),
+                    )
+                banks[(1, i)].append(acc)
+
+        def statistics_and_centre(layer, i):
+            accs = banks[(layer, i)]
+            stats = small.tile([P, len(accs), 6], F32, name="stats%d" % layer)
+            for n, acc in enumerate(accs):
+                nc.vector.bn_stats(out=stats[:, n, :], in_=acc[:])
+            mean_var = small.tile([P, 2], F32, name="mean_var")
+            nc.vector.bn_aggr(out=mean_var[:], in_=stats[:].rearrange("p n s -> p (n s)"))
+            var_eps = small.tile([P, 1], F32, name="var_eps")
+            nc.gpsimd.tensor_scalar(
+                out=var_eps[:], in0=mean_var[:, 1:2], scalar1=EPS, scalar2=1.0, op0=ALU.add, op1=ALU.mult
+            )
+            rstd = small.tile([P, 1], F32, name="rstd")
+            nc.gpsimd.tensor_tensor(out=rstd[:], in0=var_eps[:], in1=minus_half[:], op=ALU.pow)
+            v = rows.tile([P, len(accs) * BANK], F32, name="pre%d" % layer)
+            for n, acc in enumerate(accs):
+                n_cols = slice(n * BANK, (n + 1) * BANK)
+                nc.vector.scalar_tensor_tensor(
+                    out=v[:, n_cols],
+                    in0=acc[:],
+                    scalar=mean_var[:, 0:1],
+                    in1=gain[layer][:, n_cols],
+                    op0=ALU.subtract,
+                    op1=ALU.mult,
+                )
+            rstd_of[(layer, i)] = rstd
+            pre[(layer, i)] = v
+
+        def scale_shift_and_cap(layer, i):
+            v = pre[(layer, i)]
+            nc.vector.scalar_tensor_tensor(
+                out=v[:], in0=v[:], scalar=rstd_of[(layer, i)][:], in1=shift[layer][:], op0=ALU.mult, op1=ALU.add
+            )
+            a = rows.tile(list(v.shape), F32, name="act%d" % layer)
+            nc.gpsimd.tensor_scalar(out=a[:], in0=v[:], scalar1=CAP, scalar2=-CAP, op0=ALU.min, op1=ALU.max)
+            act[(layer, i)] = a
+
+        def exp_pass(layer, i):
+            a = act[(layer, i)]
+            nc.scalar.activation(out=a[:], in_=a[:], func=ACT.Exp)
+
+        def ln_pass(layer, i):
+            a = act[(layer, i)]
+            nc.scalar.activation(out=a[:], in_=a[:], func=ACT.Ln, bias=one[:])
+
+        def tanh_pass(layer, i):
+            a = act[(layer, i)]
+            nc.scalar.activation(out=a[:], in_=a[:], func=ACT.Tanh)
+
+        def hidden_rows(i):
+            h = stage.tile([P, D_HID], BF16, name="hidden")
+            nc.vector.tensor_tensor(out=h[:], in0=pre[(1, i)][:], in1=act[(1, i)][:], op=ALU.mult)
+            turned = psum.tile([P, PASSES_2, 2, P], F32, name="turned")
+            for g in range(PASSES_2):
+                turn(turned[:, g, :, :], h[:].bitcast(F32), g)
+            grouped = stage.tile([P, PASSES_2 * P * PACK], BF16, name="h_grouped", align_bytes=64)
+            nc.scalar.copy(
+                out=grouped[:].bitcast(F32).rearrange("p (g r u) -> p g r u", g=PASSES_2, u=2),
+                in_=turned[:].rearrange("p g u r -> p g r u"),
+            )
+            h_grouped[i] = grouped
+
+        def second_layer(i):
+            nc.vector.quantize_mx(
+                out=h_codes[:, i, :].bitcast(FP8X4), scales=h_scales[:, i, :], in_=h_grouped[i][:]
+            )
+            acc = psum.tile([P, BANK], F32, name="u2")
+            for g in range(PASSES_2):
+                g_cols = slice(g * P, (g + 1) * P)
+                nc.tensor.matmul_mx(
+                    out=acc[:],
+                    lhsT=h_codes[:, i, g_cols].bitcast(FP8X4),
+                    lhsT_scale=h_scales[:, i, g_cols],
+                    rhs=w2_codes[:, g, :].bitcast(FP8X4),
+                    rhs_scale=w2_scales[:, g, :],
+                    start=(g == 0),
+                    stop=(g == PASSES_2 - 1),
+                )
+            banks[(2, i)] = [acc]
+
+        def store_rows(i):
+            result = small.tile([P, D_OUT], F32, name="result")
+            nc.vector.tensor_tensor(out=result[:], in0=pre[(2, i)][:], in1=act[(2, i)][:], op=ALU.mult)
+            nc.sync.dma_start(out=out[i * P : (i + 1) * P, :], in_=result[:])
+
+        def member(group, s):
+            if group is None or s < 0 or s >= CHUNK:
+                return None
+            return group[1] * CHUNK + s
+
+        quantise_x_pair(0, turn_x_pair(0))
+        first_layer(0)
+        first_layer(1)
+
+        groups = [(1, c) for c in range(N_CHUNKS)] + [(2, c) for c in range(N_CHUNKS)]
+        for r in range(len(groups) + 1):
+            made = groups[r] if r < len(groups) else None
+            done = groups[r - 1] if r >= 1 else None
+            for s in range(CHUNK + LAG + 1):
+                i = member(done, s)
+                if i is not None:
+                    ln_pass(done[0], i)
+
+                if made is not None and made[0] == 1:
+                    i = member(made, s)
+                    if i is not None:
+                        if i + 1 < N_PAIRS:
+                            x_grouped = turn_x_pair(i + 1)
+                        statistics_and_centre(1, i)
+                        if i + 1 < N_PAIRS:
+                            quantise_x_pair(i + 1, x_grouped)
+                        if i + 2 < N_TILES:
+                            first_layer(i + 2)
+                    i = member(made, s - 1)
+                    if i is not None:
+                        scale_shift_and_cap(1, i)
+
+                if made is not None and made[0] == 2:
+                    i = member(made, s)
+                    if i is not None:
+                        hidden_rows(i)
+                    i = member(made, s - 1)
+                    if i is not None:
+                        second_layer(i)
+                    i = member(made, s - 2)
+                    if i is not None:
+                        statistics_and_centre(2, i)
+                    i = member(made, s - 3)
+                    if i is not None:
+                        scale_shift_and_cap(2, i)
+
+                i = member(done, s - LAG)
+                if i is not None:
+                    tanh_pass(done[0], i)
+                i = member(made, s - LAG)
+                if i is not None:
+                    exp_pass(made[0], i)
+                i = member(done, s - LAG - 1)
+                if i is not None and done[0] == 2:
+                    store_rows(i)

@@ -42,7 +42,6 @@ def tile_autoencoder_pa_kernel(
         small = ctx.enter_context(tc.tile_pool(name="small", bufs=4))
         rows = ctx.enter_context(tc.tile_pool(name="rows", bufs=N_TILES))
         psum = ctx.enter_context(tc.psum_pool(name="psum", bufs=2))
-        ctx.enter_context(tc.manual_schedule())
 
         identity = keep.tile([P, P], F32, name="identity")
         make_identity(nc, identity[:])
@@ -180,7 +179,7 @@ def tile_autoencoder_pa_kernel(
                 out=v[:], in0=v[:], scalar=rstd_of[(layer, i)][:], in1=shift[layer][:], op0=ALU.mult, op1=ALU.add
             )
             a = rows.tile(list(v.shape), F32, name="act%d" % layer)
-            nc.gpsimd.tensor_scalar(out=a[:], in0=v[:], scalar1=CAP, scalar2=-CAP, op0=ALU.min, op1=ALU.max)
+            nc.vector.tensor_scalar_min(out=a[:], in0=v[:], scalar1=CAP)
             act[(layer, i)] = a
 
         def exp_pass(layer, i):
@@ -197,7 +196,7 @@ def tile_autoencoder_pa_kernel(
 
         def hidden_rows(i):
             h = stage.tile([P, D_HID], BF16, name="hidden")
-            nc.vector.tensor_tensor(out=h[:], in0=pre[(1, i)][:], in1=act[(1, i)][:], op=ALU.mult)
+            nc.gpsimd.tensor_tensor(out=h[:], in0=pre[(1, i)][:], in1=act[(1, i)][:], op=ALU.mult)
             turned = psum.tile([P, PASSES_2, 2, P], F32, name="turned")
             for g in range(PASSES_2):
                 turn(turned[:, g, :, :], h[:].bitcast(F32), g)

@@ -42,6 +42,7 @@ def tile_autoencoder_pa_kernel(
         small = ctx.enter_context(tc.tile_pool(name="small", bufs=4))
         rows = ctx.enter_context(tc.tile_pool(name="rows", bufs=N_TILES))
         psum = ctx.enter_context(tc.psum_pool(name="psum", bufs=2))
+        ctx.enter_context(tc.manual_schedule())
 
         identity = keep.tile([P, P], F32, name="identity")
         make_identity(nc, identity[:])
@@ -196,7 +197,7 @@ def tile_autoencoder_pa_kernel(
 
         def hidden_rows(i):
             h = stage.tile([P, D_HID], BF16, name="hidden")
-            nc.gpsimd.tensor_tensor(out=h[:], in0=pre[(1, i)][:], in1=act[(1, i)][:], op=ALU.mult)
+            nc.vector.tensor_tensor(out=h[:], in0=pre[(1, i)][:], in1=act[(1, i)][:], op=ALU.mult)
             turned = psum.tile([P, PASSES_2, 2, P], F32, name="turned")
             for g in range(PASSES_2):
                 turn(turned[:, g, :, :], h[:].bitcast(F32), g)

@@ -24,12 +24,12 @@ PASSES_2 = D_HID // K_PASS
 WORDS = K_PASS // 2
 CHUNK = 4
 N_CHUNKS = N_TILES // CHUNK
-LAG = CHUNK - 1
+LAG = CHUNK
 EPS = 1e-5
 CAP = 40.0
 FLOPS = 2 * BATCH * D_IN * D_HID + 2 * BATCH * D_HID * D_OUT
 
-assert LAG == 3
+assert LAG == 4
 
 
 def tile_autoencoder_pa_kernel(
@@ -38,7 +38,7 @@ def tile_autoencoder_pa_kernel(
     nc = tc.nc
     with ExitStack() as ctx:
         keep = ctx.enter_context(tc.tile_pool(name="keep", bufs=1))
-        stage = ctx.enter_context(tc.tile_pool(name="stage", bufs=2))
+        stage = ctx.enter_context(tc.tile_pool(name="stage", bufs=3))
         small = ctx.enter_context(tc.tile_pool(name="small", bufs=4))
         rows = ctx.enter_context(tc.tile_pool(name="rows", bufs=N_TILES))
         psum = ctx.enter_context(tc.psum_pool(name="psum", bufs=2))
@@ -83,12 +83,12 @@ def tile_autoencoder_pa_kernel(
                 in_=words[g].rearrange("p n t -> p (n t)").bitcast(I32),
             )
 
-        load_x(0)
-        load_x(1)
+        for i in range(4):
+            load_x(i)
         load_scales(w1_scales, W1_scales)
         for g in range(PASSES_1):
             load_codes(w1_codes, W1_words, g)
-        for i in range(2, N_TILES):
+        for i in range(4, N_TILES):
             load_x(i)
         load_scales(w2_scales, W2_scales)
         for g in range(PASSES_2):
@@ -236,7 +236,8 @@ def tile_autoencoder_pa_kernel(
                 return None
             return group[1] * CHUNK + s
 
-        quantise_x_pair(0, turn_x_pair(0))
+        x_grouped = {0: turn_x_pair(0), 1: turn_x_pair(1)}
+        quantise_x_pair(0, x_grouped[0])
         first_layer(0)
         first_layer(1)
 
@@ -244,45 +245,36 @@ def tile_autoencoder_pa_kernel(
         for r in range(len(groups) + 1):
             made = groups[r] if r < len(groups) else None
             done = groups[r - 1] if r >= 1 else None
-            for s in range(CHUNK + LAG + 1):
-                i = member(done, s)
-                if i is not None:
-                    ln_pass(done[0], i)
-
+            for s in range(CHUNK + LAG + 4):
                 if made is not None and made[0] == 1:
                     i = member(made, s)
                     if i is not None:
-                        if i + 1 < N_PAIRS:
-                            x_grouped = turn_x_pair(i + 1)
+                        if i + 2 < N_PAIRS:
+                            x_grouped[i + 2] = turn_x_pair(i + 2)
                         statistics_and_centre(1, i)
+                    if member(made, s - 1) is not None:
+                        scale_shift_and_cap(1, member(made, s - 1))
+                    if i is not None:
                         if i + 1 < N_PAIRS:
-                            quantise_x_pair(i + 1, x_grouped)
+                            quantise_x_pair(i + 1, x_grouped[i + 1])
                         if i + 2 < N_TILES:
                             first_layer(i + 2)
-                    i = member(made, s - 1)
-                    if i is not None:
-                        scale_shift_and_cap(1, i)
 
                 if made is not None and made[0] == 2:
-                    i = member(made, s)
-                    if i is not None:
-                        hidden_rows(i)
-                    i = member(made, s - 1)
-                    if i is not None:
-                        second_layer(i)
-                    i = member(made, s - 2)
-                    if i is not None:
-                        statistics_and_centre(2, i)
-                    i = member(made, s - 3)
-                    if i is not None:
-                        scale_shift_and_cap(2, i)
+                    if member(made, s) is not None:
+                        hidden_rows(member(made, s))
+                    if member(made, s - 2) is not None:
+                        second_layer(member(made, s - 2))
+                    if member(made, s - 3) is not None:
+                        statistics_and_centre(2, member(made, s - 3))
+                    if member(made, s - 4) is not None:
+                        scale_shift_and_cap(2, member(made, s - 4))
 
-                i = member(done, s - LAG)
-                if i is not None:
-                    tanh_pass(done[0], i)
-                i = member(made, s - LAG)
-                if i is not None:
-                    exp_pass(made[0], i)
-                i = member(done, s - LAG - 1)
-                if i is not None and done[0] == 2:
-                    store_rows(i)
+                if member(done, s) is not None:
+                    ln_pass(done[0], member(done, s))
+                if member(done, s - LAG) is not None:
+                    tanh_pass(done[0], member(done, s - LAG))
+                if member(made, s - LAG) is not None:
+                    exp_pass(made[0], member(made, s - LAG))
+                if done is not None and done[0] == 2 and member(done, s - LAG - 3) is not None:
+                    store_rows(member(done, s - LAG - 3))

@@ -51,12 +51,17 @@ def tile_autoencoder_pa_kernel(
         minus_half = keep.tile([P, 1], F32, name="minus_half")
         nc.gpsimd.memset(minus_half[:], -0.5)
 
+        all_ones = keep.tile([P, P], BF16, name="all_ones")
+        nc.gpsimd.memset(all_ones[:], 1.0)
+
         gain = {1: keep.tile([P, D_HID], BF16, name="gain1"), 2: keep.tile([P, D_OUT], BF16, name="gain2")}
         shift = {1: keep.tile([P, D_HID], BF16, name="shift1"), 2: keep.tile([P, D_OUT], BF16, name="shift2")}
-        nc.gpsimd.dma_start(out=gain[1][:], in_=g1.partition_broadcast(P))
-        nc.gpsimd.dma_start(out=shift[1][:], in_=b1.partition_broadcast(P))
-        nc.gpsimd.dma_start(out=gain[2][:], in_=g2.partition_broadcast(P))
-        nc.gpsimd.dma_start(out=shift[2][:], in_=b2.partition_broadcast(P))
+        def spread(name, everywhere):
+            for n in range(everywhere.shape[1] // BANK):
+                n_cols = slice(n * BANK, (n + 1) * BANK)
+                repeated = psum.tile([P, BANK], F32, name="turned")
+                nc.tensor.matmul(out=repeated[:], lhsT=all_ones[:], rhs=lone_rows[name][:, n_cols], start=True, stop=True)
+                nc.scalar.copy(out=everywhere[:, n_cols], in_=repeated[:])
 
         w1_codes = keep.tile([P, PASSES_1, D_HID], U32, name="w1_codes", align_bytes=64)
         w1_scales = keep.tile([P, PASSES_1, D_HID], U8, name="w1_scales", align_bytes=64)
@@ -64,6 +69,11 @@ def tile_autoencoder_pa_kernel(
         w2_scales = keep.tile([P, PASSES_2, D_OUT], U8, name="w2_scales", align_bytes=64)
         nc.vector.memset(w1_scales[:].rearrange("p g n -> p (g n)").bitcast(I32), 0)
         nc.vector.memset(w2_scales[:].rearrange("p g n -> p (g n)").bitcast(I32), 0)
+        lone_rows = {}
+        for name, vector in (("g1", g1), ("b1", b1), ("g2", g2), ("b2", b2)):
+            lone_rows[name] = keep.tile([P, vector.shape[0]], BF16, name="row_" + name)
+            nc.vector.memset(lone_rows[name][:].bitcast(I32), 0)
+            nc.scalar.dma_start(out=lone_rows[name][0:1, :], in_=vector.rearrange("(o n) -> o n", o=1))
 
         x_sb = keep.tile([P, N_TILES, D_IN], BF16, name="x_sb")
 
@@ -237,9 +247,13 @@ def tile_autoencoder_pa_kernel(
             return group[1] * CHUNK + s
 
         x_grouped = {0: turn_x_pair(0), 1: turn_x_pair(1)}
+        spread("g1", gain[1])
+        spread("b1", shift[1])
         quantise_x_pair(0, x_grouped[0])
         first_layer(0)
         first_layer(1)
+        spread("g2", gain[2])
+        spread("b2", shift[2])
 
         groups = [(1, c) for c in range(N_CHUNKS)] + [(2, c) for c in range(N_CHUNKS)]
         for r in range(len(groups) + 1):

@@ -42,7 +42,6 @@ def tile_autoencoder_pa_kernel(
         small = ctx.enter_context(tc.tile_pool(name="small", bufs=4))
         rows = ctx.enter_context(tc.tile_pool(name="rows", bufs=N_TILES))
         psum = ctx.enter_context(tc.psum_pool(name="psum", bufs=2))
-        ctx.enter_context(tc.manual_schedule())
 
         identity = keep.tile([P, P], F32, name="identity")
         make_identity(nc, identity[:])
@@ -59,7 +58,7 @@ def tile_autoencoder_pa_kernel(
         def spread(name, everywhere):
             for n in range(everywhere.shape[1] // BANK):
                 n_cols = slice(n * BANK, (n + 1) * BANK)
-                repeated = psum.tile([P, BANK], F32, name="turned")
+                repeated = psum.tile([P, BANK], F32, name="u2")
                 nc.tensor.matmul(out=repeated[:], lhsT=all_ones[:], rhs=lone_rows[name][:, n_cols], start=True, stop=True)
                 nc.scalar.copy(out=everywhere[:, n_cols], in_=repeated[:])
 

@@ -42,6 +42,7 @@ def tile_autoencoder_pa_kernel(
         small = ctx.enter_context(tc.tile_pool(name="small", bufs=4))
         rows = ctx.enter_context(tc.tile_pool(name="rows", bufs=N_TILES))
         psum = ctx.enter_context(tc.psum_pool(name="psum", bufs=2))
+        ctx.enter_context(tc.manual_schedule())
 
         identity = keep.tile([P, P], F32, name="identity")
         make_identity(nc, identity[:])

@@ -26,7 +26,7 @@ CHUNK = 4
 N_CHUNKS = N_TILES // CHUNK
 LAG = CHUNK
 EPS = 1e-5
-CAP = 40.0
+TINY = 1e-15
 FLOPS = 2 * BATCH * D_IN * D_HID + 2 * BATCH * D_HID * D_OUT
 
 assert LAG == 4
@@ -46,8 +46,9 @@ def tile_autoencoder_pa_kernel(
 
         identity = keep.tile([P, P], F32, name="identity")
         make_identity(nc, identity[:])
-        one = keep.tile([P, 1], F32, name="one")
-        nc.gpsimd.memset(one[:], 1.0)
+        tiny = keep.tile([P, 1], F32, name="tiny")
+        nc.gpsimd.memset(tiny[:], TINY)
+        warm = keep.tile([P, 1], F32, name="warm")
         minus_half = keep.tile([P, 1], F32, name="minus_half")
         nc.gpsimd.memset(minus_half[:], -0.5)
 
@@ -184,26 +185,28 @@ def tile_autoencoder_pa_kernel(
             rstd_of[(layer, i)] = rstd
             pre[(layer, i)] = v
 
-        def scale_shift_and_cap(layer, i):
+        def scale_and_shift(layer, i):
             v = pre[(layer, i)]
             nc.vector.scalar_tensor_tensor(
                 out=v[:], in0=v[:], scalar=rstd_of[(layer, i)][:], in1=shift[layer][:], op0=ALU.mult, op1=ALU.add
             )
-            a = rows.tile(list(v.shape), F32, name="act%d" % layer)
-            nc.vector.tensor_scalar_min(out=a[:], in0=v[:], scalar1=CAP)
-            act[(layer, i)] = a
 
-        def exp_pass(layer, i):
-            a = act[(layer, i)]
-            nc.scalar.activation(out=a[:], in_=a[:], func=ACT.Exp)
+        def load_sigmoid_table():
+            nc.scalar.activation(out=warm[:], in_=tiny[:], func=ACT.Sigmoid)
+
+        def sigmoid_pass(layer, i):
+            v = pre[(layer, i)]
+            a = rows.tile(list(v.shape), F32, name="act%d" % layer)
+            nc.scalar.activation(out=a[:], in_=v[:], func=ACT.Sigmoid, scale=-1.0)
+            act[(layer, i)] = a
 
         def ln_pass(layer, i):
             a = act[(layer, i)]
-            nc.scalar.activation(out=a[:], in_=a[:], func=ACT.Ln, bias=one[:])
+            nc.scalar.activation(out=a[:], in_=a[:], func=ACT.Ln, bias=tiny[:])
 
         def tanh_pass(layer, i):
             a = act[(layer, i)]
-            nc.scalar.activation(out=a[:], in_=a[:], func=ACT.Tanh)
+            nc.scalar.activation(out=a[:], in_=a[:], func=ACT.Tanh, scale=-1.0)
 
         def hidden_rows(i):
             h = stage.tile([P, D_HID], BF16, name="hidden")
@@ -267,7 +270,7 @@ def tile_autoencoder_pa_kernel(
                             x_grouped[i + 2] = turn_x_pair(i + 2)
                         statistics_and_centre(1, i)
                     if member(made, s - 1) is not None:
-                        scale_shift_and_cap(1, member(made, s - 1))
+                        scale_and_shift(1, member(made, s - 1))
                     if i is not None:
                         if i + 1 < N_PAIRS:
                             quantise_x_pair(i + 1, x_grouped[i + 1])
@@ -282,13 +285,15 @@ def tile_autoencoder_pa_kernel(
                     if member(made, s - 3) is not None:
                         statistics_and_centre(2, member(made, s - 3))
                     if member(made, s - 4) is not None:
-                        scale_shift_and_cap(2, member(made, s - 4))
+                        scale_and_shift(2, member(made, s - 4))
 
                 if member(done, s) is not None:
                     ln_pass(done[0], member(done, s))
+                if s == LAG:
+                    load_sigmoid_table()
                 if member(done, s - LAG) is not None:
                     tanh_pass(done[0], member(done, s - LAG))
                 if member(made, s - LAG) is not None:
-                    exp_pass(made[0], member(made, s - LAG))
+                    sigmoid_pass(made[0], member(made, s - LAG))
                 if done is not None and done[0] == 2 and member(done, s - LAG - 3) is not None:
                     store_rows(member(done, s - LAG - 3))

@@ -22,14 +22,12 @@ N_PAIRS = N_TILES // 2
 PASSES_1 = D_IN // K_PASS
 PASSES_2 = D_HID // K_PASS
 WORDS = K_PASS // 2
-CHUNK = 4
-N_CHUNKS = N_TILES // CHUNK
-LAG = CHUNK
+QUANTISE_BEFORE = [0, 3, 1, 1, 1, 0, 0, 0]
+QUANTISE_BEHIND = [0, 0, 2, 1, 0, 0, 0, 0]
+GROUP = 4
 EPS = 1e-5
 TINY = 1e-15
 FLOPS = 2 * BATCH * D_IN * D_HID + 2 * BATCH * D_HID * D_OUT
-
-assert LAG == 4
 
 
 def tile_autoencoder_pa_kernel(
@@ -41,7 +39,7 @@ def tile_autoencoder_pa_kernel(
         stage = ctx.enter_context(tc.tile_pool(name="stage", bufs=3))
         small = ctx.enter_context(tc.tile_pool(name="small", bufs=4))
         rows = ctx.enter_context(tc.tile_pool(name="rows", bufs=N_TILES))
-        psum = ctx.enter_context(tc.psum_pool(name="psum", bufs=2))
+        psum = ctx.enter_context(tc.psum_pool(name="psum", bufs=4))
         ctx.enter_context(tc.manual_schedule())
 
         identity = keep.tile([P, P], F32, name="identity")
@@ -57,11 +55,19 @@ def tile_autoencoder_pa_kernel(
 
         gain = {1: keep.tile([P, D_HID], BF16, name="gain1"), 2: keep.tile([P, D_OUT], BF16, name="gain2")}
         shift = {1: keep.tile([P, D_HID], BF16, name="shift1"), 2: keep.tile([P, D_OUT], BF16, name="shift2")}
-        def spread(name, everywhere):
-            for n in range(everywhere.shape[1] // BANK):
-                n_cols = slice(n * BANK, (n + 1) * BANK)
-                repeated = psum.tile([P, BANK], F32, name="u2")
-                nc.tensor.matmul(out=repeated[:], lhsT=all_ones[:], rhs=lone_rows[name][:, n_cols], start=True, stop=True)
+
+        def turned_order(columns):
+            return columns.rearrange("r (p t) -> r t p", t=PACK)
+
+        def spread(name, layer, everywhere, n):
+            n_cols = slice(n * BANK, (n + 1) * BANK)
+            repeated = psum.tile([P, BANK], F32, name="turned")
+            nc.tensor.matmul(out=repeated[:], lhsT=all_ones[:], rhs=lone_rows[name][:, n_cols], start=True, stop=True)
+            if layer == 1:
+                nc.scalar.copy(
+                    out=everywhere[:, n_cols].rearrange("r (t p) -> r t p", t=PACK), in_=turned_order(repeated[:])
+                )
+            else:
                 nc.scalar.copy(out=everywhere[:, n_cols], in_=repeated[:])
 
         w1_codes = keep.tile([P, PASSES_1, D_HID], U32, name="w1_codes", align_bytes=64)
@@ -94,12 +100,12 @@ def tile_autoencoder_pa_kernel(
                 in_=words[g].rearrange("p n t -> p (n t)").bitcast(I32),
             )
 
-        for i in range(4):
+        for i in range(2):
             load_x(i)
         load_scales(w1_scales, W1_scales)
         for g in range(PASSES_1):
             load_codes(w1_codes, W1_words, g)
-        for i in range(4, N_TILES):
+        for i in range(2, N_TILES):
             load_x(i)
         load_scales(w2_scales, W2_scales)
         for g in range(PASSES_2):
@@ -111,41 +117,40 @@ def tile_autoencoder_pa_kernel(
         h_scales = keep.tile([P, N_TILES, PASSES_2 * P], U8, name="h_scales", align_bytes=64)
 
         banks = {}
-        rstd_of = {}
+        stats_of, mean_of, rstd_of = {}, {}, {}
         pre = {}
         act = {}
-        h_grouped = {}
+        factor = {}
+        hidden = {}
+        x_grouped = {}
 
-        def turn(bank_block, words, g):
-            for u in range(2):
-                nc.tensor.transpose(
-                    bank_block[:, u, :], words[:, WORDS * g + u : WORDS * (g + 1) : 2], identity[:]
-                )
+        def turn_x(k, g):
+            if g == 0:
+                grouped = stage.tile([P, PASSES_1, 2 * P * PACK], BF16, name="x_grouped", align_bytes=64)
+                x_grouped[k] = grouped
+            turned = psum.tile([P, 2, 2, P], F32, name="turned")
+            for j in range(2):
+                words = x_sb[:, 2 * k + j, :].bitcast(F32)
+                for u in range(2):
+                    nc.tensor.transpose(
+                        turned[:, j, u, :], words[:, WORDS * g + u : WORDS * (g + 1) : 2], identity[:]
+                    )
+            nc.scalar.copy(
+                out=x_grouped[k][:, g, :].bitcast(F32).rearrange("p (j r u) -> p j r u", j=2, u=2),
+                in_=turned[:].rearrange("p j u r -> p j r u"),
+            )
 
-        def turn_x_pair(k):
-            grouped = stage.tile([P, PASSES_1, 2 * P * PACK], BF16, name="x_grouped", align_bytes=64)
-            for g in range(PASSES_1):
-                turned = psum.tile([P, 2, 2, P], F32, name="turned")
-                for j in range(2):
-                    turn(turned[:, j, :, :], x_sb[:, 2 * k + j, :].bitcast(F32), g)
-                nc.scalar.copy(
-                    out=grouped[:, g, :].bitcast(F32).rearrange("p (j r u) -> p j r u", j=2, u=2),
-                    in_=turned[:].rearrange("p j u r -> p j r u"),
-                )
-            return grouped
-
-        def quantise_x_pair(k, grouped):
-            for g in range(PASSES_1):
-                nc.vector.quantize_mx(
-                    out=x_codes[:, k, g, :].bitcast(FP8X4), scales=x_scales[:, k, g, :], in_=grouped[:, g, :]
-                )
+        def quantise_x(k, g):
+            nc.vector.quantize_mx(
+                out=x_codes[:, k, g, :].bitcast(FP8X4), scales=x_scales[:, k, g, :], in_=x_grouped[k][:, g, :]
+            )
 
         def first_layer(i):
             tile_cols = slice((i % 2) * P, (i % 2 + 1) * P)
             banks[(1, i)] = []
             for n in range(D_HID // BANK):
                 n_cols = slice(n * BANK, (n + 1) * BANK)
-                acc = psum.tile([P, BANK], F32, name="u1_%d" % n)
+                acc = psum.tile([P, BANK], F32, name="acc")
                 for g in range(PASSES_1):
                     nc.tensor.matmul_mx(
                         out=acc[:],
@@ -158,31 +163,38 @@ def tile_autoencoder_pa_kernel(
                     )
                 banks[(1, i)].append(acc)
 
-        def statistics_and_centre(layer, i):
+        def bank_statistics(layer, i):
             accs = banks[(layer, i)]
             stats = small.tile([P, len(accs), 6], F32, name="stats%d" % layer)
             for n, acc in enumerate(accs):
                 nc.vector.bn_stats(out=stats[:, n, :], in_=acc[:])
+            stats_of[(layer, i)] = stats
+
+        def row_statistics(layer, i):
             mean_var = small.tile([P, 2], F32, name="mean_var")
-            nc.vector.bn_aggr(out=mean_var[:], in_=stats[:].rearrange("p n s -> p (n s)"))
+            nc.vector.bn_aggr(out=mean_var[:], in_=stats_of[(layer, i)][:].rearrange("p n s -> p (n s)"))
             var_eps = small.tile([P, 1], F32, name="var_eps")
             nc.gpsimd.tensor_scalar(
                 out=var_eps[:], in0=mean_var[:, 1:2], scalar1=EPS, scalar2=1.0, op0=ALU.add, op1=ALU.mult
             )
             rstd = small.tile([P, 1], F32, name="rstd")
             nc.gpsimd.tensor_tensor(out=rstd[:], in0=var_eps[:], in1=minus_half[:], op=ALU.pow)
+            mean_of[(layer, i)] = mean_var[:, 0:1]
+            rstd_of[(layer, i)] = rstd
+
+        def centre(layer, i):
+            accs = banks[(layer, i)]
             v = rows.tile([P, len(accs) * BANK], F32, name="pre%d" % layer)
             for n, acc in enumerate(accs):
                 n_cols = slice(n * BANK, (n + 1) * BANK)
+                u, v_cols, g_cols = acc[:], v[:, n_cols], gain[layer][:, n_cols]
+                if layer == 1:
+                    u = turned_order(u)
+                    v_cols = v_cols.rearrange("r (t p) -> r t p", t=PACK)
+                    g_cols = g_cols.rearrange("r (t p) -> r t p", t=PACK)
                 nc.vector.scalar_tensor_tensor(
-                    out=v[:, n_cols],
-                    in0=acc[:],
-                    scalar=mean_var[:, 0:1],
-                    in1=gain[layer][:, n_cols],
-                    op0=ALU.subtract,
-                    op1=ALU.mult,
+                    out=v_cols, in0=u, scalar=mean_of[(layer, i)], in1=g_cols, op0=ALU.subtract, op1=ALU.mult
                 )
-            rstd_of[(layer, i)] = rstd
             pre[(layer, i)] = v
 
         def scale_and_shift(layer, i):
@@ -196,7 +208,7 @@ def tile_autoencoder_pa_kernel(
 
         def sigmoid_pass(layer, i):
             v = pre[(layer, i)]
-            a = rows.tile(list(v.shape), F32, name="act%d" % layer)
+            a = rows.tile(list(v.shape), F32, name="act%d" % layer, bufs=6)
             nc.scalar.activation(out=a[:], in_=v[:], func=ACT.Sigmoid, scale=-1.0)
             act[(layer, i)] = a
 
@@ -204,28 +216,49 @@ def tile_autoencoder_pa_kernel(
             a = act[(layer, i)]
             nc.scalar.activation(out=a[:], in_=a[:], func=ACT.Ln, bias=tiny[:])
 
-        def tanh_pass(layer, i):
-            a = act[(layer, i)]
+        def tanh_pass(i):
+            a = act[(2, i)]
             nc.scalar.activation(out=a[:], in_=a[:], func=ACT.Tanh, scale=-1.0)
 
-        def hidden_rows(i):
-            h = stage.tile([P, D_HID], BF16, name="hidden")
-            nc.vector.tensor_tensor(out=h[:], in0=pre[(1, i)][:], in1=act[(1, i)][:], op=ALU.mult)
-            turned = psum.tile([P, PASSES_2, 2, P], F32, name="turned")
+        def turn(rows_tile, g, tag):
+            bank = psum.tile([P, PACK, P], F32, name=tag)
+            for t in range(PACK):
+                first = g * K_PASS + t * P
+                nc.tensor.transpose(bank[:, t, :], rows_tile[:, first : first + P], identity[:])
+            return bank
+
+        def turned_tanh_pass(i):
+            m = rows.tile([P, D_HID], F32, name="factor", bufs=GROUP)
             for g in range(PASSES_2):
-                turn(turned[:, g, :, :], h[:].bitcast(F32), g)
-            grouped = stage.tile([P, PASSES_2 * P * PACK], BF16, name="h_grouped", align_bytes=64)
-            nc.scalar.copy(
-                out=grouped[:].bitcast(F32).rearrange("p (g r u) -> p g r u", g=PASSES_2, u=2),
-                in_=turned[:].rearrange("p g u r -> p g r u"),
+                bank = turn(act[(1, i)], g, "turned")
+                nc.scalar.activation(
+                    out=m[:, g * BANK : (g + 1) * BANK].rearrange("p (r t) -> p r t", t=PACK),
+                    in_=bank[:].rearrange("p t r -> p r t"),
+                    func=ACT.Tanh,
+                    scale=-1.0,
+                )
+            factor[i] = m
+
+        def turn_v(i):
+            banks[("v", i)] = [turn(pre[(1, i)], g, "acc") for g in range(PASSES_2)]
+
+        def hidden_rows(i, g):
+            if g == 0:
+                h = stage.tile([P, D_HID], BF16, name="hidden", align_bytes=64)
+                hidden[i] = h
+            g_cols = slice(g * BANK, (g + 1) * BANK)
+            nc.vector.tensor_tensor(
+                out=hidden[i][:, g_cols].rearrange("p (r t) -> p r t", t=PACK),
+                in0=banks[("v", i)][g][:].rearrange("p t r -> p r t"),
+                in1=factor[i][:, g_cols].rearrange("p (r t) -> p r t", t=PACK),
+                op=ALU.mult,
             )
-            h_grouped[i] = grouped
+
+        def quantise_hidden(i):
+            nc.vector.quantize_mx(out=h_codes[:, i, :].bitcast(FP8X4), scales=h_scales[:, i, :], in_=hidden[i][:])
 
         def second_layer(i):
-            nc.vector.quantize_mx(
-                out=h_codes[:, i, :].bitcast(FP8X4), scales=h_scales[:, i, :], in_=h_grouped[i][:]
-            )
-            acc = psum.tile([P, BANK], F32, name="u2")
+            acc = psum.tile([P, BANK], F32, name="acc")
             for g in range(PASSES_2):
                 g_cols = slice(g * P, (g + 1) * P)
                 nc.tensor.matmul_mx(
@@ -244,56 +277,89 @@ def tile_autoencoder_pa_kernel(
             nc.vector.tensor_tensor(out=result[:], in0=pre[(2, i)][:], in1=act[(2, i)][:], op=ALU.mult)
             nc.sync.dma_start(out=out[i * P : (i + 1) * P, :], in_=result[:])
 
-        def member(group, s):
-            if group is None or s < 0 or s >= CHUNK:
-                return None
-            return group[1] * CHUNK + s
-
-        x_grouped = {0: turn_x_pair(0), 1: turn_x_pair(1)}
-        spread("g1", gain[1])
-        spread("b1", shift[1])
-        quantise_x_pair(0, x_grouped[0])
+        load_sigmoid_table()
+        turn_x(0, 0)
+        spread("g1", 1, gain[1], 0)
+        turn_x(0, 1)
+        spread("g1", 1, gain[1], 1)
+        turn_x(0, 2)
+        spread("b1", 1, shift[1], 0)
+        spread("b1", 1, shift[1], 1)
+        spread("g2", 2, gain[2], 0)
+        spread("b2", 2, shift[2], 0)
+        for g in range(PASSES_1):
+            quantise_x(0, g)
         first_layer(0)
         first_layer(1)
-        spread("g2", gain[2])
-        spread("b2", shift[2])
+        for k in (1, 2):
+            for g in range(PASSES_1):
+                turn_x(k, g)
 
-        groups = [(1, c) for c in range(N_CHUNKS)] + [(2, c) for c in range(N_CHUNKS)]
-        for r in range(len(groups) + 1):
-            made = groups[r] if r < len(groups) else None
-            done = groups[r - 1] if r >= 1 else None
-            for s in range(CHUNK + LAG + 4):
-                if made is not None and made[0] == 1:
-                    i = member(made, s)
-                    if i is not None:
-                        if i + 2 < N_PAIRS:
-                            x_grouped[i + 2] = turn_x_pair(i + 2)
-                        statistics_and_centre(1, i)
-                    if member(made, s - 1) is not None:
-                        scale_and_shift(1, member(made, s - 1))
-                    if i is not None:
-                        if i + 1 < N_PAIRS:
-                            quantise_x_pair(i + 1, x_grouped[i + 1])
-                        if i + 2 < N_TILES:
-                            first_layer(i + 2)
+        to_quantise = [(k, g) for k in (1, 2, 3) for g in range(PASSES_1)]
+        for i in range(N_TILES):
+            bank_statistics(1, i)
+            if i >= 1:
+                scale_and_shift(1, i - 1)
+                if i - 1 < GROUP:
+                    sigmoid_pass(1, i - 1)
+            row_statistics(1, i)
+            for k, g in to_quantise[:QUANTISE_BEFORE[i]]:
+                quantise_x(k, g)
+            to_quantise = to_quantise[QUANTISE_BEFORE[i]:]
+            if i == 1:
+                first_layer(2)
+                for g in range(PASSES_1):
+                    turn_x(3, g)
+            centre(1, i)
+            for k, g in to_quantise[:QUANTISE_BEHIND[i]]:
+                quantise_x(k, g)
+            to_quantise = to_quantise[QUANTISE_BEHIND[i]:]
+            if 1 <= i and i + 2 < N_TILES:
+                first_layer(i + 2)
 
-                if made is not None and made[0] == 2:
-                    if member(made, s) is not None:
-                        hidden_rows(member(made, s))
-                    if member(made, s - 2) is not None:
-                        second_layer(member(made, s - 2))
-                    if member(made, s - 3) is not None:
-                        statistics_and_centre(2, member(made, s - 3))
-                    if member(made, s - 4) is not None:
-                        scale_and_shift(2, member(made, s - 4))
-
-                if member(done, s) is not None:
-                    ln_pass(done[0], member(done, s))
-                if s == LAG:
-                    load_sigmoid_table()
-                if member(done, s - LAG) is not None:
-                    tanh_pass(done[0], member(done, s - LAG))
-                if member(made, s - LAG) is not None:
-                    sigmoid_pass(made[0], member(made, s - LAG))
-                if done is not None and done[0] == 2 and member(done, s - LAG - 3) is not None:
-                    store_rows(member(done, s - LAG - 3))
+        groups = [range(c * GROUP, (c + 1) * GROUP) for c in range(N_TILES // GROUP)]
+        for i in groups[0]:
+            ln_pass(1, i)
+        load_sigmoid_table()
+        for c, group in enumerate(groups):
+            turned_tanh_pass(group[0])
+            for j, i in enumerate(group):
+                if j + 1 < GROUP:
+                    turned_tanh_pass(group[j + 1])
+                turn_v(i)
+                hidden_rows(i, 0)
+                if i == 0:
+                    scale_and_shift(1, N_TILES - 1)
+                if j >= 1:
+                    quantise_hidden(group[j - 1])
+                hidden_rows(i, 1)
+                if j >= 2:
+                    second_layer(group[j - 2])
+            bank_statistics(2, group[0])
+            row_statistics(2, group[0])
+            quantise_hidden(group[-1])
+            second_layer(group[-2])
+            second_layer(group[-1])
+            for j in range(1, GROUP + 2):
+                if j < GROUP:
+                    bank_statistics(2, group[j])
+                    row_statistics(2, group[j])
+                if 0 <= j - 1 < GROUP:
+                    centre(2, group[j - 1])
+                if 0 <= j - 2 < GROUP:
+                    scale_and_shift(2, group[j - 2])
+            if c + 1 < len(groups):
+                for i in groups[c + 1]:
+                    sigmoid_pass(1, i)
+                for i in groups[c + 1]:
+                    ln_pass(1, i)
+                load_sigmoid_table()
+        for c, group in enumerate(groups):
+            for i in group:
+                sigmoid_pass(2, i)
+            for i in group:
+                ln_pass(2, i)
+            load_sigmoid_table()
+            for i in group:
+                tanh_pass(i)
+                store_rows(i)

@@ -22,9 +22,10 @@ N_PAIRS = N_TILES // 2
 PASSES_1 = D_IN // K_PASS
 PASSES_2 = D_HID // K_PASS
 WORDS = K_PASS // 2
-QUANTISE_BEFORE = [0, 3, 1, 1, 1, 0, 0, 0]
-QUANTISE_BEHIND = [0, 0, 2, 1, 0, 0, 0, 0]
+QUANTISE = [0, 3, 3, 0, 3, 0, 0, 0]
 GROUP = 4
+EARLY = 2
+WARM_UP = 8
 EPS = 1e-5
 TINY = 1e-15
 FLOPS = 2 * BATCH * D_IN * D_HID + 2 * BATCH * D_HID * D_OUT
@@ -42,6 +43,10 @@ def tile_autoencoder_pa_kernel(
         psum = ctx.enter_context(tc.psum_pool(name="psum", bufs=4))
         ctx.enter_context(tc.manual_schedule())
 
+        all_ones = keep.tile([P, P], BF16, name="all_ones")
+        nc.vector.memset(all_ones[:], 1.0)
+        zeros = keep.tile([P, BANK], BF16, name="zeros")
+        nc.vector.memset(zeros[:].bitcast(I32), 0)
         identity = keep.tile([P, P], F32, name="identity")
         make_identity(nc, identity[:])
         tiny = keep.tile([P, 1], F32, name="tiny")
@@ -49,9 +54,6 @@ def tile_autoencoder_pa_kernel(
         warm = keep.tile([P, 1], F32, name="warm")
         minus_half = keep.tile([P, 1], F32, name="minus_half")
         nc.gpsimd.memset(minus_half[:], -0.5)
-
-        all_ones = keep.tile([P, P], BF16, name="all_ones")
-        nc.gpsimd.memset(all_ones[:], 1.0)
 
         gain = {1: keep.tile([P, D_HID], BF16, name="gain1"), 2: keep.tile([P, D_OUT], BF16, name="gain2")}
         shift = {1: keep.tile([P, D_HID], BF16, name="shift1"), 2: keep.tile([P, D_OUT], BF16, name="shift2")}
@@ -278,11 +280,13 @@ def tile_autoencoder_pa_kernel(
             nc.sync.dma_start(out=out[i * P : (i + 1) * P, :], in_=result[:])
 
         load_sigmoid_table()
-        turn_x(0, 0)
+        for w in range(WARM_UP):
+            unread = psum.tile([P, BANK], F32, name="acc")
+            nc.tensor.matmul(out=unread[:], lhsT=all_ones[:], rhs=zeros[:], start=True, stop=True)
+        for g in range(PASSES_1):
+            turn_x(0, g)
         spread("g1", 1, gain[1], 0)
-        turn_x(0, 1)
         spread("g1", 1, gain[1], 1)
-        turn_x(0, 2)
         spread("b1", 1, shift[1], 0)
         spread("b1", 1, shift[1], 1)
         spread("g2", 2, gain[2], 0)
@@ -298,33 +302,42 @@ def tile_autoencoder_pa_kernel(
         to_quantise = [(k, g) for k in (1, 2, 3) for g in range(PASSES_1)]
         for i in range(N_TILES):
             bank_statistics(1, i)
-            if i >= 1:
+            if i >= 1 and i != GROUP:
                 scale_and_shift(1, i - 1)
                 if i - 1 < GROUP:
                     sigmoid_pass(1, i - 1)
             row_statistics(1, i)
-            for k, g in to_quantise[:QUANTISE_BEFORE[i]]:
+            for k, g in to_quantise[: QUANTISE[i]]:
                 quantise_x(k, g)
-            to_quantise = to_quantise[QUANTISE_BEFORE[i]:]
+            to_quantise = to_quantise[QUANTISE[i] :]
             if i == 1:
                 first_layer(2)
                 for g in range(PASSES_1):
                     turn_x(3, g)
             centre(1, i)
-            for k, g in to_quantise[:QUANTISE_BEHIND[i]]:
-                quantise_x(k, g)
-            to_quantise = to_quantise[QUANTISE_BEHIND[i]:]
+            if i == GROUP - 1:
+                scale_and_shift(1, i)
+                sigmoid_pass(1, i)
             if 1 <= i and i + 2 < N_TILES:
                 first_layer(i + 2)
+            if i == EARLY:
+                for e in range(EARLY):
+                    ln_pass(1, e)
+                load_sigmoid_table()
+                for e in range(EARLY):
+                    turned_tanh_pass(e)
 
         groups = [range(c * GROUP, (c + 1) * GROUP) for c in range(N_TILES // GROUP)]
-        for i in groups[0]:
+        for i in groups[0][EARLY:]:
             ln_pass(1, i)
         load_sigmoid_table()
+        for i in groups[0][EARLY:]:
+            turned_tanh_pass(i)
         for c, group in enumerate(groups):
-            turned_tanh_pass(group[0])
+            if c >= 1:
+                turned_tanh_pass(group[0])
             for j, i in enumerate(group):
-                if j + 1 < GROUP:
+                if c >= 1 and j + 1 < GROUP:
                     turned_tanh_pass(group[j + 1])
                 turn_v(i)
                 hidden_rows(i, 0)

@@ -41,7 +41,7 @@ def tile_autoencoder_pa_kernel(
         small = ctx.enter_context(tc.tile_pool(name="small", bufs=4))
         rows = ctx.enter_context(tc.tile_pool(name="rows", bufs=N_TILES))
         psum = ctx.enter_context(tc.psum_pool(name="psum", bufs=4))
-        ctx.enter_context(tc.manual_schedule())
+        ctx.enter_context(tc.manual_schedule(engines={mybir.EngineType.Activation, mybir.EngineType.PE}))
 
         all_ones = keep.tile([P, P], BF16, name="all_ones")
         nc.vector.memset(all_ones[:], 1.0)
@@ -51,6 +51,8 @@ def tile_autoencoder_pa_kernel(
         make_identity(nc, identity[:])
         tiny = keep.tile([P, 1], F32, name="tiny")
         nc.gpsimd.memset(tiny[:], TINY)
+        half = keep.tile([P, 1], F32, name="half")
+        nc.gpsimd.memset(half[:], 0.5)
         warm = keep.tile([P, 1], F32, name="warm")
         minus_half = keep.tile([P, 1], F32, name="minus_half")
         nc.gpsimd.memset(minus_half[:], -0.5)
@@ -279,6 +281,24 @@ def tile_autoencoder_pa_kernel(
             nc.vector.tensor_tensor(out=result[:], in0=pre[(2, i)][:], in1=act[(2, i)][:], op=ALU.mult)
             nc.sync.dma_start(out=out[i * P : (i + 1) * P, :], in_=result[:])
 
+        def load_root_table():
+            nc.scalar.activation(out=warm[:], in_=half[:], func=ACT.Abs_reciprocal_sqrt)
+
+        def square(i):
+            a = act[(2, i)]
+            nc.vector.tensor_tensor(out=a[:], in0=a[:], in1=a[:], op=ALU.mult)
+
+        def root_pass(i):
+            a = act[(2, i)]
+            nc.scalar.activation(out=a[:], in_=a[:], func=ACT.Abs_reciprocal_sqrt, scale=0.5, bias=half[:])
+
+        def store_last_rows(i):
+            result = small.tile([P, D_OUT], F32, name="result")
+            nc.vector.scalar_tensor_tensor(
+                out=result[:], in0=act[(2, i)][:], scalar=1.0, in1=pre[(2, i)][:], op0=ALU.subtract, op1=ALU.mult
+            )
+            nc.sync.dma_start(out=out[i * P : (i + 1) * P, :], in_=result[:])
+
         load_sigmoid_table()
         for w in range(WARM_UP):
             unread = psum.tile([P, BANK], F32, name="acc")
@@ -367,7 +387,7 @@ def tile_autoencoder_pa_kernel(
                 for i in groups[c + 1]:
                     ln_pass(1, i)
                 load_sigmoid_table()
-        for c, group in enumerate(groups):
+        for group in groups[:-1]:
             for i in group:
                 sigmoid_pass(2, i)
             for i in group:
@@ -376,3 +396,15 @@ def tile_autoencoder_pa_kernel(
             for i in group:
                 tanh_pass(i)
                 store_rows(i)
+        for i in groups[-1]:
+            sigmoid_pass(2, i)
+            square(i)
+        load_root_table()
+        for i in groups[-1]:
+            root_pass(i)
+        for j, i in enumerate(groups[-1]):
+            if j < GROUP // 2:
+                square(i)
+            else:
+                nc.scalar.activation(out=act[(2, i)][:], in_=act[(2, i)][:], func=ACT.Square)
+            store_last_rows(i)

@@ -98,22 +98,24 @@ def tile_autoencoder_pa_kernel(
                     in_=scales[:, 4 * quadrant : 4 * quadrant + 4, :].rearrange("g r n -> r g n").bitcast(I32),
                 )
 
-        def load_codes(codes, words, g):
+        def load_codes(codes, words, g, n):
+            n_cols = slice(n * BANK, (n + 1) * BANK)
             nc.sync.dma_start(
-                out=codes[:, g, :].bitcast(I32),
-                in_=words[g].rearrange("p n t -> p (n t)").bitcast(I32),
+                out=codes[:, g, n_cols].bitcast(I32),
+                in_=words[g, :, n_cols, :].rearrange("p n t -> p (n t)").bitcast(I32),
             )
 
         for i in range(2):
             load_x(i)
         load_scales(w1_scales, W1_scales)
-        for g in range(PASSES_1):
-            load_codes(w1_codes, W1_words, g)
+        for n in range(D_HID // BANK):
+            for g in range(PASSES_1):
+                load_codes(w1_codes, W1_words, g, n)
         for i in range(2, N_TILES):
             load_x(i)
         load_scales(w2_scales, W2_scales)
         for g in range(PASSES_2):
-            load_codes(w2_codes, W2_words, g)
+            load_codes(w2_codes, W2_words, g, 0)
 
         x_codes = keep.tile([P, N_PAIRS, PASSES_1, 2 * P], U32, name="x_codes", align_bytes=64)
         x_scales = keep.tile([P, N_PAIRS, PASSES_1, 2 * P], U8, name="x_scales", align_bytes=64)
@@ -292,12 +294,20 @@ def tile_autoencoder_pa_kernel(
             a = act[(2, i)]
             nc.scalar.activation(out=a[:], in_=a[:], func=ACT.Abs_reciprocal_sqrt, scale=0.5, bias=half[:])
 
-        def store_last_rows(i):
-            result = small.tile([P, D_OUT], F32, name="result")
-            nc.vector.scalar_tensor_tensor(
-                out=result[:], in0=act[(2, i)][:], scalar=1.0, in1=pre[(2, i)][:], op0=ALU.subtract, op1=ALU.mult
-            )
-            nc.sync.dma_start(out=out[i * P : (i + 1) * P, :], in_=result[:])
+        def finish_last_rows(i, engine, parts):
+            width = D_OUT // parts
+            for n in range(parts):
+                n_cols = slice(n * width, (n + 1) * width)
+                a = act[(2, i)][:, n_cols]
+                if engine is nc.scalar:
+                    nc.scalar.activation(out=a, in_=a, func=ACT.Square)
+                else:
+                    nc.vector.tensor_tensor(out=a, in0=a, in1=a, op=ALU.mult)
+                result = small.tile([P, D_OUT], F32, name="result")
+                nc.vector.scalar_tensor_tensor(
+                    out=result[:, :width], in0=a, scalar=1.0, in1=pre[(2, i)][:, n_cols], op0=ALU.subtract, op1=ALU.mult
+                )
+                nc.sync.dma_start(out=out[i * P : (i + 1) * P, n_cols], in_=result[:, :width])
 
         load_sigmoid_table()
         for w in range(WARM_UP):
@@ -343,16 +353,22 @@ def tile_autoencoder_pa_kernel(
             if i == EARLY:
                 for e in range(EARLY):
                     ln_pass(1, e)
-                load_sigmoid_table()
+            if i == GROUP - 1:
                 for e in range(EARLY):
                     turned_tanh_pass(e)
 
         groups = [range(c * GROUP, (c + 1) * GROUP) for c in range(N_TILES // GROUP)]
         for i in groups[0][EARLY:]:
             ln_pass(1, i)
-        load_sigmoid_table()
+        for i in groups[1][:-1]:
+            sigmoid_pass(1, i)
         for i in groups[0][EARLY:]:
             turned_tanh_pass(i)
+        scale_and_shift(1, N_TILES - 1)
+        sigmoid_pass(1, N_TILES - 1)
+        for i in groups[1]:
+            ln_pass(1, i)
+        load_sigmoid_table()
         for c, group in enumerate(groups):
             if c >= 1:
                 turned_tanh_pass(group[0])
@@ -361,8 +377,6 @@ def tile_autoencoder_pa_kernel(
                     turned_tanh_pass(group[j + 1])
                 turn_v(i)
                 hidden_rows(i, 0)
-                if i == 0:
-                    scale_and_shift(1, N_TILES - 1)
                 if j >= 1:
                     quantise_hidden(group[j - 1])
                 hidden_rows(i, 1)
@@ -381,12 +395,6 @@ def tile_autoencoder_pa_kernel(
                     centre(2, group[j - 1])
                 if 0 <= j - 2 < GROUP:
                     scale_and_shift(2, group[j - 2])
-            if c + 1 < len(groups):
-                for i in groups[c + 1]:
-                    sigmoid_pass(1, i)
-                for i in groups[c + 1]:
-                    ln_pass(1, i)
-                load_sigmoid_table()
         for group in groups[:-1]:
             for i in group:
                 sigmoid_pass(2, i)
@@ -403,8 +411,4 @@ def tile_autoencoder_pa_kernel(
         for i in groups[-1]:
             root_pass(i)
         for j, i in enumerate(groups[-1]):
-            if j < GROUP // 2:
-                square(i)
-            else:
-                nc.scalar.activation(out=act[(2, i)][:], in_=act[(2, i)][:], func=ACT.Square)
-            store_last_rows(i)
+            finish_last_rows(i, nc.vector if j < GROUP // 2 else nc.scalar, 2 if j == GROUP - 1 else 1)

@@ -25,7 +25,7 @@ WORDS = K_PASS // 2
 QUANTISE = [0, 3, 3, 0, 3, 0, 0, 0]
 GROUP = 4
 EARLY = 2
-WARM_UP = 8
+WARM_UP = 0
 EPS = 1e-5
 TINY = 1e-15
 FLOPS = 2 * BATCH * D_IN * D_HID + 2 * BATCH * D_HID * D_OUT

from contextlib import ExitStack

import concourse.mybir as mybir
from concourse.masks import make_identity

F32 = mybir.dt.float32
BF16 = mybir.dt.bfloat16
I32 = mybir.dt.int32
U32 = mybir.dt.uint32
U8 = mybir.dt.uint8
FP8X4 = mybir.dt.float8_e4m3fn_x4
ALU = mybir.AluOpType
ACT = mybir.ActivationFunctionType

P = 128
PACK = 4
K_PASS = P * PACK
BANK = 512
BATCH, D_IN, D_HID, D_OUT = 1024, 1536, 1024, 512
N_TILES = BATCH // P
N_PAIRS = N_TILES // 2
PASSES_1 = D_IN // K_PASS
PASSES_2 = D_HID // K_PASS
WORDS = K_PASS // 2
QUANTISE = [0, 3, 3, 0, 3, 0, 0, 0]
GROUP = 4
EARLY = 2
WARM_UP = 0
EPS = 1e-5
TINY = 1e-15
FLOPS = 2 * BATCH * D_IN * D_HID + 2 * BATCH * D_HID * D_OUT


def tile_autoencoder_pa_kernel(
    tc, x, W1_words, W1_scales, g1, b1, W2_words, W2_scales, g2, b2, out
):
    nc = tc.nc
    with ExitStack() as ctx:
        keep = ctx.enter_context(tc.tile_pool(name="keep", bufs=1))
        stage = ctx.enter_context(tc.tile_pool(name="stage", bufs=3))
        small = ctx.enter_context(tc.tile_pool(name="small", bufs=4))
        rows = ctx.enter_context(tc.tile_pool(name="rows", bufs=N_TILES))
        psum = ctx.enter_context(tc.psum_pool(name="psum", bufs=4))
        ctx.enter_context(tc.manual_schedule(engines={mybir.EngineType.Activation, mybir.EngineType.PE}))

        all_ones = keep.tile([P, P], BF16, name="all_ones")
        nc.vector.memset(all_ones[:], 1.0)
        zeros = keep.tile([P, BANK], BF16, name="zeros")
        nc.vector.memset(zeros[:].bitcast(I32), 0)
        identity = keep.tile([P, P], F32, name="identity")
        make_identity(nc, identity[:])
        tiny = keep.tile([P, 1], F32, name="tiny")
        nc.gpsimd.memset(tiny[:], TINY)
        half = keep.tile([P, 1], F32, name="half")
        nc.gpsimd.memset(half[:], 0.5)
        warm = keep.tile([P, 1], F32, name="warm")
        minus_half = keep.tile([P, 1], F32, name="minus_half")
        nc.gpsimd.memset(minus_half[:], -0.5)

        gain = {1: keep.tile([P, D_HID], BF16, name="gain1"), 2: keep.tile([P, D_OUT], BF16, name="gain2")}
        shift = {1: keep.tile([P, D_HID], BF16, name="shift1"), 2: keep.tile([P, D_OUT], BF16, name="shift2")}

        def turned_order(columns):
            return columns.rearrange("r (p t) -> r t p", t=PACK)

        def spread(name, layer, everywhere, n):
            n_cols = slice(n * BANK, (n + 1) * BANK)
            repeated = psum.tile([P, BANK], F32, name="turned")
            nc.tensor.matmul(out=repeated[:], lhsT=all_ones[:], rhs=lone_rows[name][:, n_cols], start=True, stop=True)
            if layer == 1:
                nc.scalar.copy(
                    out=everywhere[:, n_cols].rearrange("r (t p) -> r t p", t=PACK), in_=turned_order(repeated[:])
                )
            else:
                nc.scalar.copy(out=everywhere[:, n_cols], in_=repeated[:])

        w1_codes = keep.tile([P, PASSES_1, D_HID], U32, name="w1_codes", align_bytes=64)
        w1_scales = keep.tile([P, PASSES_1, D_HID], U8, name="w1_scales", align_bytes=64)
        w2_codes = keep.tile([P, PASSES_2, D_OUT], U32, name="w2_codes", align_bytes=64)
        w2_scales = keep.tile([P, PASSES_2, D_OUT], U8, name="w2_scales", align_bytes=64)
        nc.vector.memset(w1_scales[:].rearrange("p g n -> p (g n)").bitcast(I32), 0)
        nc.vector.memset(w2_scales[:].rearrange("p g n -> p (g n)").bitcast(I32), 0)
        lone_rows = {}
        for name, vector in (("g1", g1), ("b1", b1), ("g2", g2), ("b2", b2)):
            lone_rows[name] = keep.tile([P, vector.shape[0]], BF16, name="row_" + name)
            nc.vector.memset(lone_rows[name][:].bitcast(I32), 0)
            nc.scalar.dma_start(out=lone_rows[name][0:1, :], in_=vector.rearrange("(o n) -> o n", o=1))

        x_sb = keep.tile([P, N_TILES, D_IN], BF16, name="x_sb")

        def load_x(i):
            nc.sync.dma_start(out=x_sb[:, i, :], in_=x[i * P : (i + 1) * P, :])

        def load_scales(plane, scales):
            for quadrant in range(4):
                nc.sync.dma_start(
                    out=plane[32 * quadrant : 32 * quadrant + 4, :, :].bitcast(I32),
                    in_=scales[:, 4 * quadrant : 4 * quadrant + 4, :].rearrange("g r n -> r g n").bitcast(I32),
                )

        def load_codes(codes, words, g, n):
            n_cols = slice(n * BANK, (n + 1) * BANK)
            nc.sync.dma_start(
                out=codes[:, g, n_cols].bitcast(I32),
                in_=words[g, :, n_cols, :].rearrange("p n t -> p (n t)").bitcast(I32),
            )

        for i in range(2):
            load_x(i)
        load_scales(w1_scales, W1_scales)
        for n in range(D_HID // BANK):
            for g in range(PASSES_1):
                load_codes(w1_codes, W1_words, g, n)
        for i in range(2, N_TILES):
            load_x(i)
        load_scales(w2_scales, W2_scales)
        for g in range(PASSES_2):
            load_codes(w2_codes, W2_words, g, 0)

        x_codes = keep.tile([P, N_PAIRS, PASSES_1, 2 * P], U32, name="x_codes", align_bytes=64)
        x_scales = keep.tile([P, N_PAIRS, PASSES_1, 2 * P], U8, name="x_scales", align_bytes=64)
        h_codes = keep.tile([P, N_TILES, PASSES_2 * P], U32, name="h_codes", align_bytes=64)
        h_scales = keep.tile([P, N_TILES, PASSES_2 * P], U8, name="h_scales", align_bytes=64)

        banks = {}
        stats_of, mean_of, rstd_of = {}, {}, {}
        pre = {}
        act = {}
        factor = {}
        hidden = {}
        x_grouped = {}

        def turn_x(k, g):
            if g == 0:
                grouped = stage.tile([P, PASSES_1, 2 * P * PACK], BF16, name="x_grouped", align_bytes=64)
                x_grouped[k] = grouped
            turned = psum.tile([P, 2, 2, P], F32, name="turned")
            for j in range(2):
                words = x_sb[:, 2 * k + j, :].bitcast(F32)
                for u in range(2):
                    nc.tensor.transpose(
                        turned[:, j, u, :], words[:, WORDS * g + u : WORDS * (g + 1) : 2], identity[:]
                    )
            nc.scalar.copy(
                out=x_grouped[k][:, g, :].bitcast(F32).rearrange("p (j r u) -> p j r u", j=2, u=2),
                in_=turned[:].rearrange("p j u r -> p j r u"),
            )

        def quantise_x(k, g):
            nc.vector.quantize_mx(
                out=x_codes[:, k, g, :].bitcast(FP8X4), scales=x_scales[:, k, g, :], in_=x_grouped[k][:, g, :]
            )

        def first_layer(i):
            tile_cols = slice((i % 2) * P, (i % 2 + 1) * P)
            banks[(1, i)] = []
            for n in range(D_HID // BANK):
                n_cols = slice(n * BANK, (n + 1) * BANK)
                acc = psum.tile([P, BANK], F32, name="acc")
                for g in range(PASSES_1):
                    nc.tensor.matmul_mx(
                        out=acc[:],
                        lhsT=x_codes[:, i // 2, g, tile_cols].bitcast(FP8X4),
                        lhsT_scale=x_scales[:, i // 2, g, tile_cols],
                        rhs=w1_codes[:, g, n_cols].bitcast(FP8X4),
                        rhs_scale=w1_scales[:, g, n_cols],
                        start=(g == 0),
                        stop=(g == PASSES_1 - 1),
                    )
                banks[(1, i)].append(acc)

        def bank_statistics(layer, i):
            accs = banks[(layer, i)]
            stats = small.tile([P, len(accs), 6], F32, name="stats%d" % layer)
            for n, acc in enumerate(accs):
                nc.vector.bn_stats(out=stats[:, n, :], in_=acc[:])
            stats_of[(layer, i)] = stats

        def row_statistics(layer, i):
            mean_var = small.tile([P, 2], F32, name="mean_var")
            nc.vector.bn_aggr(out=mean_var[:], in_=stats_of[(layer, i)][:].rearrange("p n s -> p (n s)"))
            var_eps = small.tile([P, 1], F32, name="var_eps")
            nc.gpsimd.tensor_scalar(
                out=var_eps[:], in0=mean_var[:, 1:2], scalar1=EPS, scalar2=1.0, op0=ALU.add, op1=ALU.mult
            )
            rstd = small.tile([P, 1], F32, name="rstd")
            nc.gpsimd.tensor_tensor(out=rstd[:], in0=var_eps[:], in1=minus_half[:], op=ALU.pow)
            mean_of[(layer, i)] = mean_var[:, 0:1]
            rstd_of[(layer, i)] = rstd

        def centre(layer, i):
            accs = banks[(layer, i)]
            v = rows.tile([P, len(accs) * BANK], F32, name="pre%d" % layer)
            for n, acc in enumerate(accs):
                n_cols = slice(n * BANK, (n + 1) * BANK)
                u, v_cols, g_cols = acc[:], v[:, n_cols], gain[layer][:, n_cols]
                if layer == 1:
                    u = turned_order(u)
                    v_cols = v_cols.rearrange("r (t p) -> r t p", t=PACK)
                    g_cols = g_cols.rearrange("r (t p) -> r t p", t=PACK)
                nc.vector.scalar_tensor_tensor(
                    out=v_cols, in0=u, scalar=mean_of[(layer, i)], in1=g_cols, op0=ALU.subtract, op1=ALU.mult
                )
            pre[(layer, i)] = v

        def scale_and_shift(layer, i):
            v = pre[(layer, i)]
            nc.vector.scalar_tensor_tensor(
                out=v[:], in0=v[:], scalar=rstd_of[(layer, i)][:], in1=shift[layer][:], op0=ALU.mult, op1=ALU.add
            )

        def load_sigmoid_table():
            nc.scalar.activation(out=warm[:], in_=tiny[:], func=ACT.Sigmoid)

        def sigmoid_pass(layer, i):
            v = pre[(layer, i)]
            a = rows.tile(list(v.shape), F32, name="act%d" % layer, bufs=6)
            nc.scalar.activation(out=a[:], in_=v[:], func=ACT.Sigmoid, scale=-1.0)
            act[(layer, i)] = a

        def ln_pass(layer, i):
            a = act[(layer, i)]
            nc.scalar.activation(out=a[:], in_=a[:], func=ACT.Ln, bias=tiny[:])

        def tanh_pass(i):
            a = act[(2, i)]
            nc.scalar.activation(out=a[:], in_=a[:], func=ACT.Tanh, scale=-1.0)

        def turn(rows_tile, g, tag):
            bank = psum.tile([P, PACK, P], F32, name=tag)
            for t in range(PACK):
                first = g * K_PASS + t * P
                nc.tensor.transpose(bank[:, t, :], rows_tile[:, first : first + P], identity[:])
            return bank

        def turned_tanh_pass(i):
            m = rows.tile([P, D_HID], F32, name="factor", bufs=GROUP)
            for g in range(PASSES_2):
                bank = turn(act[(1, i)], g, "turned")
                nc.scalar.activation(
                    out=m[:, g * BANK : (g + 1) * BANK].rearrange("p (r t) -> p r t", t=PACK),
                    in_=bank[:].rearrange("p t r -> p r t"),
                    func=ACT.Tanh,
                    scale=-1.0,
                )
            factor[i] = m

        def turn_v(i):
            banks[("v", i)] = [turn(pre[(1, i)], g, "acc") for g in range(PASSES_2)]

        def hidden_rows(i, g):
            if g == 0:
                h = stage.tile([P, D_HID], BF16, name="hidden", align_bytes=64)
                hidden[i] = h
            g_cols = slice(g * BANK, (g + 1) * BANK)
            nc.vector.tensor_tensor(
                out=hidden[i][:, g_cols].rearrange("p (r t) -> p r t", t=PACK),
                in0=banks[("v", i)][g][:].rearrange("p t r -> p r t"),
                in1=factor[i][:, g_cols].rearrange("p (r t) -> p r t", t=PACK),
                op=ALU.mult,
            )

        def quantise_hidden(i):
            nc.vector.quantize_mx(out=h_codes[:, i, :].bitcast(FP8X4), scales=h_scales[:, i, :], in_=hidden[i][:])

        def second_layer(i):
            acc = psum.tile([P, BANK], F32, name="acc")
            for g in range(PASSES_2):
                g_cols = slice(g * P, (g + 1) * P)
                nc.tensor.matmul_mx(
                    out=acc[:],
                    lhsT=h_codes[:, i, g_cols].bitcast(FP8X4),
                    lhsT_scale=h_scales[:, i, g_cols],
                    rhs=w2_codes[:, g, :].bitcast(FP8X4),
                    rhs_scale=w2_scales[:, g, :],
                    start=(g == 0),
                    stop=(g == PASSES_2 - 1),
                )
            banks[(2, i)] = [acc]

        def store_rows(i):
            result = small.tile([P, D_OUT], F32, name="result")
            nc.vector.tensor_tensor(out=result[:], in0=pre[(2, i)][:], in1=act[(2, i)][:], op=ALU.mult)
            nc.sync.dma_start(out=out[i * P : (i + 1) * P, :], in_=result[:])

        def load_root_table():
            nc.scalar.activation(out=warm[:], in_=half[:], func=ACT.Abs_reciprocal_sqrt)

        def square(i):
            a = act[(2, i)]
            nc.vector.tensor_tensor(out=a[:], in0=a[:], in1=a[:], op=ALU.mult)

        def root_pass(i):
            a = act[(2, i)]
            nc.scalar.activation(out=a[:], in_=a[:], func=ACT.Abs_reciprocal_sqrt, scale=0.5, bias=half[:])

        def finish_last_rows(i, engine, parts):
            width = D_OUT // parts
            for n in range(parts):
                n_cols = slice(n * width, (n + 1) * width)
                a = act[(2, i)][:, n_cols]
                if engine is nc.scalar:
                    nc.scalar.activation(out=a, in_=a, func=ACT.Square)
                else:
                    nc.vector.tensor_tensor(out=a, in0=a, in1=a, op=ALU.mult)
                result = small.tile([P, D_OUT], F32, name="result")
                nc.vector.scalar_tensor_tensor(
                    out=result[:, :width], in0=a, scalar=1.0, in1=pre[(2, i)][:, n_cols], op0=ALU.subtract, op1=ALU.mult
                )
                nc.sync.dma_start(out=out[i * P : (i + 1) * P, n_cols], in_=result[:, :width])

        load_sigmoid_table()
        for w in range(WARM_UP):
            unread = psum.tile([P, BANK], F32, name="acc")
            nc.tensor.matmul(out=unread[:], lhsT=all_ones[:], rhs=zeros[:], start=True, stop=True)
        for g in range(PASSES_1):
            turn_x(0, g)
        spread("g1", 1, gain[1], 0)
        spread("g1", 1, gain[1], 1)
        spread("b1", 1, shift[1], 0)
        spread("b1", 1, shift[1], 1)
        spread("g2", 2, gain[2], 0)
        spread("b2", 2, shift[2], 0)
        for g in range(PASSES_1):
            quantise_x(0, g)
        first_layer(0)
        first_layer(1)
        for k in (1, 2):
            for g in range(PASSES_1):
                turn_x(k, g)

        to_quantise = [(k, g) for k in (1, 2, 3) for g in range(PASSES_1)]
        for i in range(N_TILES):
            bank_statistics(1, i)
            if i >= 1 and i != GROUP:
                scale_and_shift(1, i - 1)
                if i - 1 < GROUP:
                    sigmoid_pass(1, i - 1)
            row_statistics(1, i)
            for k, g in to_quantise[: QUANTISE[i]]:
                quantise_x(k, g)
            to_quantise = to_quantise[QUANTISE[i] :]
            if i == 1:
                first_layer(2)
                for g in range(PASSES_1):
                    turn_x(3, g)
            centre(1, i)
            if i == GROUP - 1:
                scale_and_shift(1, i)
                sigmoid_pass(1, i)
            if 1 <= i and i + 2 < N_TILES:
                first_layer(i + 2)
            if i == EARLY:
                for e in range(EARLY):
                    ln_pass(1, e)
            if i == GROUP - 1:
                for e in range(EARLY):
                    turned_tanh_pass(e)

        groups = [range(c * GROUP, (c + 1) * GROUP) for c in range(N_TILES // GROUP)]
        for i in groups[0][EARLY:]:
            ln_pass(1, i)
        for i in groups[1][:-1]:
            sigmoid_pass(1, i)
        for i in groups[0][EARLY:]:
            turned_tanh_pass(i)
        scale_and_shift(1, N_TILES - 1)
        sigmoid_pass(1, N_TILES - 1)
        for i in groups[1]:
            ln_pass(1, i)
        load_sigmoid_table()
        for c, group in enumerate(groups):
            if c >= 1:
                turned_tanh_pass(group[0])
            for j, i in enumerate(group):
                if c >= 1 and j + 1 < GROUP:
                    turned_tanh_pass(group[j + 1])
                turn_v(i)
                hidden_rows(i, 0)
                if j >= 1:
                    quantise_hidden(group[j - 1])
                hidden_rows(i, 1)
                if j >= 2:
                    second_layer(group[j - 2])
            bank_statistics(2, group[0])
            row_statistics(2, group[0])
            quantise_hidden(group[-1])
            second_layer(group[-2])
            second_layer(group[-1])
            for j in range(1, GROUP + 2):
                if j < GROUP:
                    bank_statistics(2, group[j])
                    row_statistics(2, group[j])
                if 0 <= j - 1 < GROUP:
                    centre(2, group[j - 1])
                if 0 <= j - 2 < GROUP:
                    scale_and_shift(2, group[j - 2])
        for group in groups[:-1]:
            for i in group:
                sigmoid_pass(2, i)
            for i in group:
                ln_pass(2, i)
            load_sigmoid_table()
            for i in group:
                tanh_pass(i)
                store_rows(i)
        for i in groups[-1]:
            sigmoid_pass(2, i)
            square(i)
        load_root_table()
        for i in groups[-1]:
            root_pass(i)
        for j, i in enumerate(groups[-1]):
            finish_last_rows(i, nc.vector if j < GROUP // 2 else nc.scalar, 2 if j == GROUP - 1 else 1)
